import numpy as np
import ml_dtypes


def mxq(x, axis, fmt="e4m3"):
    dtype, down = {"e4m3": (ml_dtypes.float8_e4m3fn, 7), "e5m2": (ml_dtypes.float8_e5m2, 14)}[fmt]
    v = np.moveaxis(np.asarray(x, np.float32).astype(ml_dtypes.bfloat16).astype(np.float64), axis, -1)
    blocks = v.reshape(v.shape[:-1] + (-1, 32))
    amax = np.abs(blocks).max(-1, keepdims=True)
    byte = np.maximum(np.where(amax > 0, np.frexp(amax)[1] - 1 + 127, 0) - down, 1)
    scale = np.exp2(byte - 127.0)
    codes = (blocks / scale).astype(np.float32).astype(dtype).astype(np.float64)
    return np.moveaxis((codes * scale).reshape(v.shape), -1, axis)


WIDE = False


def mx_kscale(k):
    if not WIDE:
        return np.ones(k)
    levels = np.array([10, -10, 5, -5, 0])
    if k % 512:
        return np.exp2(np.random.permutation(np.resize(levels, k // 32))).repeat(32)
    a = np.empty((k // 512, 16))
    for p in range(k // 512):
        a[p, :8] = np.random.permutation(np.resize(levels, 8))
        for g in range(8):
            far = levels[np.abs(levels - a[p, g]) >= 10]
            a[p, g + 8] = far[np.random.randint(len(far))]
    return np.exp2(a.ravel()).repeat(32)


BF16 = ml_dtypes.bfloat16


def bf(x):
    return np.asarray(x, np.float32).astype(BF16)


def f64(x):
    return np.asarray(x).astype(np.float64)


B, S, D, H, HD = 4, 128, 2048, 16, 128
E = H * HD
HALF = HD // 2


def rope(t, fc, fs):
    p = t.reshape(B, S, H, HALF, 2)
    tr, ti = p[..., 0], p[..., 1]
    return np.stack([tr * fc - ti * fs, tr * fs + ti * fc], axis=-1).reshape(B, S, H, HD)


def setup_inputs():
    s = mx_kscale(D)
    return {"x": bf(np.random.standard_normal((B, S, D)) * s),
            "freq_cos": bf(np.cos(np.random.standard_normal((S, HALF)))),
            "freq_sin": bf(np.sin(np.random.standard_normal((S, HALF)))),
            "wq": bf(np.random.standard_normal((E, D)) / np.sqrt(D) / s[None, :]),
            "wk": bf(np.random.standard_normal((E, D)) / np.sqrt(D) / s[None, :])}


def reference(x, freq_cos, freq_sin, wq, wk):
    xq = mxq(f64(x), 2, "e4m3")
    q = (xq @ mxq(f64(wq), 1, "e4m3").T).reshape(B, S, H, HD)
    k = (xq @ mxq(f64(wk), 1, "e4m3").T).reshape(B, S, H, HD)
    fc = f64(freq_cos)[None, :, None, :]
    fs = f64(freq_sin)[None, :, None, :]
    q_rot = rope(q, fc, fs).transpose(0, 2, 1, 3)
    k_rot = rope(k, fc, fs).transpose(0, 2, 1, 3)
    return q_rot, k_rot

@@ -1,0 +1,179 @@
+from contextlib import ExitStack
+
+import concourse.mybir as mybir
+from concourse.masks import make_identity
+
+F32 = mybir.dt.float32
+BF16 = mybir.dt.bfloat16
+U32 = mybir.dt.uint32
+U8 = mybir.dt.uint8
+FP8X4 = mybir.dt.float8_e4m3fn_x4
+MULT = mybir.AluOpType.mult
+ADD = mybir.AluOpType.add
+
+B, S, D, H, HD = 4, 128, 2048, 16, 128
+HALF = HD // 2
+P = 128
+K_PASS = 4 * P
+PASSES = D // K_PASS
+WORDS = D // 2
+SLAB = 2 * P
+SLAB_HEADS = SLAB // HD
+X_SLABS = B * S // SLAB
+W_SLABS = H * HD // SLAB
+BANK = 512
+RAW_BUFS = 12
+
+FLOPS = 2 * (B * S) * D * (2 * H * HD)
+
+
+def tile_attention_pa_kernel(tc, x, freq_cos, freq_sin, wq, wk, out_0, out_1):
+    nc = tc.nc
+
+    slabs = [x[2 * n : 2 * n + 2].rearrange("b s k -> s b k") for n in range(X_SLABS)]
+    for w in (wq, wk):
+        for n in range(W_SLABS):
+            slabs.append(w[n * SLAB : (n + 1) * SLAB, :].rearrange("(c i) k -> c i k", i=2))
+    targets = [(out, n * SLAB_HEADS) for out in (out_0, out_1) for n in range(W_SLABS)]
+
+    with ExitStack() as ctx:
+        keep = ctx.enter_context(tc.tile_pool(name="keep", bufs=1))
+        raw_pool = ctx.enter_context(tc.tile_pool(name="raw", bufs=RAW_BUFS))
+        grouped_pool = ctx.enter_context(tc.tile_pool(name="grouped", bufs=3))
+        w_pool = ctx.enter_context(tc.tile_pool(name="w_mx", bufs=3))
+        rope_pool = ctx.enter_context(tc.tile_pool(name="rope", bufs=3))
+        result_pool = ctx.enter_context(tc.tile_pool(name="result", bufs=6))
+        turned_pool = ctx.enter_context(tc.psum_pool(name="turned", bufs=4))
+        product_pool = ctx.enter_context(tc.psum_pool(name="product", bufs=4))
+        ctx.enter_context(tc.manual_schedule())
+
+        raw_tiles = {}
+        grouped_tiles = {}
+        mx_tiles = {}
+
+        def load(n):
+            raw = raw_pool.tile([P, 2 * D], BF16)
+            nc.sync.dma_start(out=raw[:].rearrange("p (r k) -> p r k", r=2), in_=slabs[n])
+            raw_tiles[n] = raw
+
+        def transpose_and_regroup(n):
+            words = raw_tiles[n][:].bitcast(F32)
+            grouped = grouped_pool.tile([P, PASSES * SLAB * 4], BF16, align_bytes=64)
+            grouped_words = grouped[:].bitcast(F32).rearrange(
+                "p (g r c u) -> p g r c u", g=PASSES, r=2, u=2
+            )
+            for g in range(PASSES):
+                turned = turned_pool.tile([P, 2, 2, P], F32)
+                for r in range(2):
+                    for u in range(2):
+                        first = r * WORDS + 2 * g * P + u
+                        nc.tensor.transpose(
+                            turned[:, r, u, :], words[:, first : first + 2 * P - 1 : 2], ident[:]
+                        )
+                nc.scalar.copy(out=grouped_words[:, g], in_=turned[:].rearrange("p r u c -> p r c u"))
+            grouped_tiles[n] = grouped
+
+        def new_mx_tiles(n):
+            pool, label = (keep, "x%d" % n) if n < X_SLABS else (w_pool, "w")
+            codes = pool.tile([P, PASSES * SLAB], U32, name=label + "_codes", align_bytes=64)
+            scales = pool.tile([P, PASSES * SLAB], U8, name=label + "_scales", align_bytes=64)
+            mx_tiles[n] = (codes, scales)
+
+        def quantise(n, half):
+            codes, scales = mx_tiles[n]
+            cols = slice(half * 2 * SLAB, (half + 1) * 2 * SLAB)
+            nc.vector.quantize_mx(
+                out=codes[:, cols].bitcast(FP8X4),
+                scales=scales[:, cols],
+                in_=grouped_tiles[n][:, half * 8 * SLAB : (half + 1) * 8 * SLAB],
+            )
+
+        def multiply(n, x_slab):
+            x_codes, x_scales = mx_tiles[x_slab]
+            w_codes, w_scales = mx_tiles[n]
+            product = product_pool.tile([P, BANK], F32)
+            for entry in range(2):
+                for g in range(PASSES):
+                    x_cols = slice(g * SLAB + entry * P, g * SLAB + (entry + 1) * P)
+                    w_cols = slice(g * SLAB, (g + 1) * SLAB)
+                    nc.tensor.matmul_mx(
+                        out=product[:, entry * SLAB : (entry + 1) * SLAB],
+                        lhsT=x_codes[:, x_cols].bitcast(FP8X4),
+                        lhsT_scale=x_scales[:, x_cols],
+                        rhs=w_codes[:, w_cols].bitcast(FP8X4),
+                        rhs_scale=w_scales[:, w_cols],
+                        start=(g == 0),
+                        stop=(g == PASSES - 1),
+                    )
+            return product
+
+        def rotate_and_store(product, x_slab, target):
+            planes = product[:].rearrange("p (b i c) -> p b i c", b=2, i=2)
+            twice = [P, 2, P, 2]
+            from_even = rope_pool.tile([P, BANK], F32)
+            nc.vector.tensor_tensor(
+                out=from_even[:].rearrange("p (b c i) -> p b c i", b=2, i=2),
+                in0=planes[:, :, 0, :].unsqueeze(3).to_broadcast(twice),
+                in1=cos_sin[:].rearrange("p (b c i) -> p b c i", b=2, i=2),
+                op=MULT,
+            )
+            from_odd = rope_pool.tile([P, BANK], F32)
+            nc.vector.tensor_tensor(
+                out=from_odd[:].rearrange("p (b c i) -> p b c i", b=2, i=2),
+                in0=planes[:, :, 1, :].unsqueeze(3).to_broadcast(twice),
+                in1=minus_sin_cos[:].rearrange("p (b c i) -> p b c i", b=2, i=2),
+                op=MULT,
+            )
+            rotated = result_pool.tile([P, BANK], F32)
+            nc.gpsimd.tensor_tensor(out=rotated[:], in0=from_even[:], in1=from_odd[:], op=ADD)
+            out, first_head = target
+            for entry in range(2):
+                nc.sync.dma_start(
+                    out=out[2 * x_slab + entry, first_head : first_head + SLAB_HEADS].rearrange(
+                        "h s d -> s h d"
+                    ),
+                    in_=rotated[:, entry * SLAB : (entry + 1) * SLAB].rearrange(
+                        "p (h d) -> p h d", h=SLAB_HEADS
+                    ),
+                )
+
+        cos_bf = keep.tile([P, HALF], BF16)
+        sin_bf = keep.tile([P, HALF], BF16)
+        nc.scalar.dma_start(out=cos_bf[:], in_=freq_cos)
+        nc.scalar.dma_start(out=sin_bf[:], in_=freq_sin)
+        for n in range(RAW_BUFS):
+            load(n)
+
+        ident = keep.tile([P, P], F32)
+        make_identity(nc, ident[:])
+
+        repeats = BANK // HD
+        cos_sin = keep.tile([P, BANK], F32)
+        minus_sin_cos = keep.tile([P, BANK], F32)
+        cos_sin_view = cos_sin[:].rearrange("p (n j i) -> p n j i", n=repeats, i=2)
+        minus_sin_cos_view = minus_sin_cos[:].rearrange("p (n j i) -> p n j i", n=repeats, i=2)
+        cos_repeated = cos_bf[:].unsqueeze(1).to_broadcast([P, repeats, HALF])
+        sin_repeated = sin_bf[:].unsqueeze(1).to_broadcast([P, repeats, HALF])
+        nc.vector.tensor_copy(out=cos_sin_view[:, :, :, 0], in_=cos_repeated)
+        nc.vector.tensor_copy(out=cos_sin_view[:, :, :, 1], in_=sin_repeated)
+        nc.vector.tensor_scalar_mul(out=minus_sin_cos_view[:, :, :, 0], in0=sin_repeated, scalar1=-1.0)
+        nc.vector.tensor_copy(out=minus_sin_cos_view[:, :, :, 1], in_=cos_repeated)
+
+        for n in range(X_SLABS + 1):
+            transpose_and_regroup(n)
+            new_mx_tiles(n)
+            quantise(n, 0)
+            quantise(n, 1)
+
+        last = len(slabs) - 1
+        for n in range(X_SLABS, len(slabs)):
+            if n - X_SLABS + RAW_BUFS <= last:
+                load(n - X_SLABS + RAW_BUFS)
+            if n < last:
+                transpose_and_regroup(n + 1)
+                new_mx_tiles(n + 1)
+            products = [multiply(n, x_slab) for x_slab in range(X_SLABS)]
+            for part in range(2):
+                if n < last:
+                    quantise(n + 1, part)
+                rotate_and_store(products[part], part, targets[n - X_SLABS])

@@ -22,6 +22,7 @@ SLAB_HEADS = SLAB // HD
 X_SLABS = B * S // SLAB
 W_SLABS = H * HD // SLAB
 BANK = 512
+ORDERED_PASSES = 2
 RAW_BUFS = 12
 
 FLOPS = 2 * (B * S) * D * (2 * H * HD)
@@ -39,6 +40,7 @@ def tile_attention_pa_kernel(tc, x, freq_cos, freq_sin, wq, wk, out_0, out_1):
     with ExitStack() as ctx:
         keep = ctx.enter_context(tc.tile_pool(name="keep", bufs=1))
         raw_pool = ctx.enter_context(tc.tile_pool(name="raw", bufs=RAW_BUFS))
+        ordered_pool = ctx.enter_context(tc.tile_pool(name="ordered", bufs=3))
         grouped_pool = ctx.enter_context(tc.tile_pool(name="grouped", bufs=3))
         w_pool = ctx.enter_context(tc.tile_pool(name="w_mx", bufs=3))
         rope_pool = ctx.enter_context(tc.tile_pool(name="rope", bufs=3))
@@ -48,6 +50,7 @@ def tile_attention_pa_kernel(tc, x, freq_cos, freq_sin, wq, wk, out_0, out_1):
         ctx.enter_context(tc.manual_schedule())
 
         raw_tiles = {}
+        ordered_tiles = {}
         grouped_tiles = {}
         mx_tiles = {}
 
@@ -55,6 +58,16 @@ def tile_attention_pa_kernel(tc, x, freq_cos, freq_sin, wq, wk, out_0, out_1):
             raw = raw_pool.tile([P, 2 * D], BF16)
             nc.sync.dma_start(out=raw[:].rearrange("p (r k) -> p r k", r=2), in_=slabs[n])
             raw_tiles[n] = raw
+
+        def order_words(n):
+            count = ORDERED_PASSES * P
+            ordered = ordered_pool.tile([P, 2 * 2 * count], F32)
+            words = raw_tiles[n][:].bitcast(F32).rearrange("p (r w) -> p r w", r=2)
+            nc.scalar.copy(
+                out=ordered[:].rearrange("p (r u c) -> p r u c", r=2, u=2),
+                in_=words[:, :, : 2 * count].rearrange("p r (c u) -> p r u c", u=2),
+            )
+            ordered_tiles[n] = ordered
 
         def transpose_and_regroup(n):
             words = raw_tiles[n][:].bitcast(F32)
@@ -66,10 +79,13 @@ def tile_attention_pa_kernel(tc, x, freq_cos, freq_sin, wq, wk, out_0, out_1):
                 turned = turned_pool.tile([P, 2, 2, P], F32)
                 for r in range(2):
                     for u in range(2):
-                        first = r * WORDS + 2 * g * P + u
-                        nc.tensor.transpose(
-                            turned[:, r, u, :], words[:, first : first + 2 * P - 1 : 2], ident[:]
-                        )
+                        if n in ordered_tiles and g < ORDERED_PASSES:
+                            first = ((2 * r + u) * ORDERED_PASSES + g) * P
+                            source = ordered_tiles[n][:, first : first + P]
+                        else:
+                            first = r * WORDS + 2 * g * P + u
+                            source = words[:, first : first + 2 * P - 1 : 2]
+                        nc.tensor.transpose(turned[:, r, u, :], source, ident[:])
                 nc.scalar.copy(out=grouped_words[:, g], in_=turned[:].rearrange("p r u c -> p r c u"))
             grouped_tiles[n] = grouped
 
@@ -172,6 +188,8 @@ def tile_attention_pa_kernel(tc, x, freq_cos, freq_sin, wq, wk, out_0, out_1):
             if n < last:
                 transpose_and_regroup(n + 1)
                 new_mx_tiles(n + 1)
+            if n + 2 <= last:
+                order_words(n + 2)
             products = [multiply(n, x_slab) for x_slab in range(X_SLABS)]
             for part in range(2):
                 if n < last:

@@ -23,7 +23,7 @@ X_SLABS = B * S // SLAB
 W_SLABS = H * HD // SLAB
 BANK = 512
 ORDERED_PASSES = 2
-RAW_BUFS = 12
+RAW_BUFS = 9
 
 FLOPS = 2 * (B * S) * D * (2 * H * HD)
 
@@ -40,11 +40,11 @@ def tile_attention_pa_kernel(tc, x, freq_cos, freq_sin, wq, wk, out_0, out_1):
     with ExitStack() as ctx:
         keep = ctx.enter_context(tc.tile_pool(name="keep", bufs=1))
         raw_pool = ctx.enter_context(tc.tile_pool(name="raw", bufs=RAW_BUFS))
-        ordered_pool = ctx.enter_context(tc.tile_pool(name="ordered", bufs=3))
+        ordered_pool = ctx.enter_context(tc.tile_pool(name="ordered", bufs=4))
         grouped_pool = ctx.enter_context(tc.tile_pool(name="grouped", bufs=3))
         w_pool = ctx.enter_context(tc.tile_pool(name="w_mx", bufs=3))
         rope_pool = ctx.enter_context(tc.tile_pool(name="rope", bufs=3))
-        result_pool = ctx.enter_context(tc.tile_pool(name="result", bufs=6))
+        result_pool = ctx.enter_context(tc.tile_pool(name="result", bufs=8))
         turned_pool = ctx.enter_context(tc.psum_pool(name="turned", bufs=4))
         product_pool = ctx.enter_context(tc.psum_pool(name="product", bufs=4))
         ctx.enter_context(tc.manual_schedule())
@@ -56,7 +56,10 @@ def tile_attention_pa_kernel(tc, x, freq_cos, freq_sin, wq, wk, out_0, out_1):
 
         def load(n):
             raw = raw_pool.tile([P, 2 * D], BF16)
-            nc.sync.dma_start(out=raw[:].rearrange("p (r k) -> p r k", r=2), in_=slabs[n])
+            rows = raw[:].rearrange("p (r k) -> p r k", r=2)
+            width = K_PASS if n == 0 else D
+            for k in range(0, D, width):
+                nc.sync.dma_start(out=rows[:, :, k : k + width], in_=slabs[n][:, :, k : k + width])
             raw_tiles[n] = raw
 
         def order_words(n):
@@ -104,16 +107,17 @@ def tile_attention_pa_kernel(tc, x, freq_cos, freq_sin, wq, wk, out_0, out_1):
                 in_=grouped_tiles[n][:, half * 8 * SLAB : (half + 1) * 8 * SLAB],
             )
 
-        def multiply(n, x_slab):
-            x_codes, x_scales = mx_tiles[x_slab]
+        def multiply(n, entries):
             w_codes, w_scales = mx_tiles[n]
             product = product_pool.tile([P, BANK], F32)
-            for entry in range(2):
+            for place, entry in enumerate(entries):
+                x_codes, x_scales = mx_tiles[entry // 2]
                 for g in range(PASSES):
-                    x_cols = slice(g * SLAB + entry * P, g * SLAB + (entry + 1) * P)
+                    x_row = g * SLAB + entry % 2 * P
+                    x_cols = slice(x_row, x_row + P)
                     w_cols = slice(g * SLAB, (g + 1) * SLAB)
                     nc.tensor.matmul_mx(
-                        out=product[:, entry * SLAB : (entry + 1) * SLAB],
+                        out=product[:, place * SLAB : (place + 1) * SLAB],
                         lhsT=x_codes[:, x_cols].bitcast(FP8X4),
                         lhsT_scale=x_scales[:, x_cols],
                         rhs=w_codes[:, w_cols].bitcast(FP8X4),
@@ -123,32 +127,34 @@ def tile_attention_pa_kernel(tc, x, freq_cos, freq_sin, wq, wk, out_0, out_1):
                     )
             return product
 
-        def rotate_and_store(product, x_slab, target):
-            planes = product[:].rearrange("p (b i c) -> p b i c", b=2, i=2)
-            twice = [P, 2, P, 2]
+        def rotate_and_store(product, entries, target, adder):
+            count = len(entries)
+            cols = count * SLAB
+            planes = product[:, :cols].rearrange("p (b i c) -> p b i c", b=count, i=2)
+            twice = [P, count, P, 2]
             from_even = rope_pool.tile([P, BANK], F32)
             nc.vector.tensor_tensor(
-                out=from_even[:].rearrange("p (b c i) -> p b c i", b=2, i=2),
+                out=from_even[:, :cols].rearrange("p (b c i) -> p b c i", b=count, i=2),
                 in0=planes[:, :, 0, :].unsqueeze(3).to_broadcast(twice),
-                in1=cos_sin[:].rearrange("p (b c i) -> p b c i", b=2, i=2),
+                in1=cos_sin[:, :cols].rearrange("p (b c i) -> p b c i", b=count, i=2),
                 op=MULT,
             )
             from_odd = rope_pool.tile([P, BANK], F32)
             nc.vector.tensor_tensor(
-                out=from_odd[:].rearrange("p (b c i) -> p b c i", b=2, i=2),
+                out=from_odd[:, :cols].rearrange("p (b c i) -> p b c i", b=count, i=2),
                 in0=planes[:, :, 1, :].unsqueeze(3).to_broadcast(twice),
-                in1=minus_sin_cos[:].rearrange("p (b c i) -> p b c i", b=2, i=2),
+                in1=minus_sin_cos[:, :cols].rearrange("p (b c i) -> p b c i", b=count, i=2),
                 op=MULT,
             )
             rotated = result_pool.tile([P, BANK], F32)
-            nc.gpsimd.tensor_tensor(out=rotated[:], in0=from_even[:], in1=from_odd[:], op=ADD)
+            adder.tensor_tensor(
+                out=rotated[:, :cols], in0=from_even[:, :cols], in1=from_odd[:, :cols], op=ADD
+            )
             out, first_head = target
-            for entry in range(2):
+            for place, entry in enumerate(entries):
                 nc.sync.dma_start(
-                    out=out[2 * x_slab + entry, first_head : first_head + SLAB_HEADS].rearrange(
-                        "h s d -> s h d"
-                    ),
-                    in_=rotated[:, entry * SLAB : (entry + 1) * SLAB].rearrange(
+                    out=out[entry, first_head : first_head + SLAB_HEADS].rearrange("h s d -> s h d"),
+                    in_=rotated[:, place * SLAB : (place + 1) * SLAB].rearrange(
                         "p (h d) -> p h d", h=SLAB_HEADS
                     ),
                 )
@@ -188,10 +194,12 @@ def tile_attention_pa_kernel(tc, x, freq_cos, freq_sin, wq, wk, out_0, out_1):
             if n < last:
                 transpose_and_regroup(n + 1)
                 new_mx_tiles(n + 1)
-            if n + 2 <= last:
-                order_words(n + 2)
-            products = [multiply(n, x_slab) for x_slab in range(X_SLABS)]
-            for part in range(2):
+            if n + 3 <= last:
+                order_words(n + 3)
+            groups = [(0, 1), (2, 3)] if n < last else [(entry,) for entry in range(B)]
+            products = [multiply(n, entries) for entries in groups]
+            for part, entries in enumerate(groups):
                 if n < last:
                     quantise(n + 1, part)
-                rotate_and_store(products[part], part, targets[n - X_SLABS])
+                adder = nc.gpsimd if n < last or part < B - 1 else nc.vector
+                rotate_and_store(products[part], entries, targets[n - X_SLABS], adder)

@@ -24,6 +24,7 @@ W_SLABS = H * HD // SLAB
 BANK = 512
 ORDERED_PASSES = 2
 RAW_BUFS = 9
+OVERLAP = 8
 
 FLOPS = 2 * (B * S) * D * (2 * H * HD)
 
@@ -43,7 +44,7 @@ def tile_attention_pa_kernel(tc, x, freq_cos, freq_sin, wq, wk, out_0, out_1):
         ordered_pool = ctx.enter_context(tc.tile_pool(name="ordered", bufs=4))
         grouped_pool = ctx.enter_context(tc.tile_pool(name="grouped", bufs=3))
         w_pool = ctx.enter_context(tc.tile_pool(name="w_mx", bufs=3))
-        rope_pool = ctx.enter_context(tc.tile_pool(name="rope", bufs=3))
+        rope_pool = ctx.enter_context(tc.tile_pool(name="rope", bufs=4))
         result_pool = ctx.enter_context(tc.tile_pool(name="result", bufs=8))
         turned_pool = ctx.enter_context(tc.psum_pool(name="turned", bufs=4))
         product_pool = ctx.enter_context(tc.psum_pool(name="product", bufs=4))
@@ -127,7 +128,7 @@ def tile_attention_pa_kernel(tc, x, freq_cos, freq_sin, wq, wk, out_0, out_1):
                     )
             return product
 
-        def rotate_and_store(product, entries, target, adder):
+        def times_tables(product, entries):
             count = len(entries)
             cols = count * SLAB
             planes = product[:, :cols].rearrange("p (b i c) -> p b i c", b=count, i=2)
@@ -146,10 +147,9 @@ def tile_attention_pa_kernel(tc, x, freq_cos, freq_sin, wq, wk, out_0, out_1):
                 in1=minus_sin_cos[:, :cols].rearrange("p (b c i) -> p b c i", b=count, i=2),
                 op=MULT,
             )
-            rotated = result_pool.tile([P, BANK], F32)
-            adder.tensor_tensor(
-                out=rotated[:, :cols], in0=from_even[:, :cols], in1=from_odd[:, :cols], op=ADD
-            )
+            return from_even, from_odd
+
+        def store(rotated, entries, target):
             out, first_head = target
             for place, entry in enumerate(entries):
                 nc.sync.dma_start(
@@ -158,6 +158,27 @@ def tile_attention_pa_kernel(tc, x, freq_cos, freq_sin, wq, wk, out_0, out_1):
                         "p (h d) -> p h d", h=SLAB_HEADS
                     ),
                 )
+
+        def add_shared(factors, entries, target):
+            from_even, from_odd = factors
+            rotated = result_pool.tile([P, BANK], F32)
+            for adder, cols in (
+                (nc.vector, slice(0, SLAB + OVERLAP)),
+                (nc.gpsimd, slice(SLAB, BANK)),
+            ):
+                adder.tensor_tensor(
+                    out=rotated[:, cols], in0=from_even[:, cols], in1=from_odd[:, cols], op=ADD
+                )
+            store(rotated, entries, target)
+
+        def add_alone(adder, factors, entries, target):
+            from_even, from_odd = factors
+            rotated = result_pool.tile([P, BANK], F32)
+            cols = slice(0, len(entries) * SLAB)
+            adder.tensor_tensor(
+                out=rotated[:, cols], in0=from_even[:, cols], in1=from_odd[:, cols], op=ADD
+            )
+            store(rotated, entries, target)
 
         cos_bf = keep.tile([P, HALF], BF16)
         sin_bf = keep.tile([P, HALF], BF16)
@@ -188,6 +209,7 @@ def tile_attention_pa_kernel(tc, x, freq_cos, freq_sin, wq, wk, out_0, out_1):
             quantise(n, 1)
 
         last = len(slabs) - 1
+        waiting = None
         for n in range(X_SLABS, len(slabs)):
             if n - X_SLABS + RAW_BUFS <= last:
                 load(n - X_SLABS + RAW_BUFS)
@@ -196,10 +218,17 @@ def tile_attention_pa_kernel(tc, x, freq_cos, freq_sin, wq, wk, out_0, out_1):
                 new_mx_tiles(n + 1)
             if n + 3 <= last:
                 order_words(n + 3)
+            target = targets[n - X_SLABS]
             groups = [(0, 1), (2, 3)] if n < last else [(entry,) for entry in range(B)]
             products = [multiply(n, entries) for entries in groups]
             for part, entries in enumerate(groups):
                 if n < last:
                     quantise(n + 1, part)
-                adder = nc.gpsimd if n < last or part < B - 1 else nc.vector
-                rotate_and_store(products[part], entries, targets[n - X_SLABS], adder)
+                if waiting:
+                    add_shared(*waiting)
+                    waiting = None
+                factors = times_tables(products[part], entries)
+                if n < last:
+                    waiting = (factors, entries, target)
+                else:
+                    add_alone(nc.gpsimd if part < B - 1 else nc.vector, factors, entries, target)

@@ -22,7 +22,8 @@ SLAB_HEADS = SLAB // HD
 X_SLABS = B * S // SLAB
 W_SLABS = H * HD // SLAB
 BANK = 512
-ORDERED_PASSES = 2
+ORDERED_PASSES = 3
+FIRST_ORDERED = X_SLABS + 3
 RAW_BUFS = 9
 OVERLAP = 8
 
@@ -63,18 +64,19 @@ def tile_attention_pa_kernel(tc, x, freq_cos, freq_sin, wq, wk, out_0, out_1):
                 nc.sync.dma_start(out=rows[:, :, k : k + width], in_=slabs[n][:, :, k : k + width])
             raw_tiles[n] = raw
 
-        def order_words(n):
-            count = ORDERED_PASSES * P
-            ordered = ordered_pool.tile([P, 2 * 2 * count], F32)
+        def order_words(n, copy, pool, count):
+            columns = count * P
+            ordered = pool.tile([P, 2 * 2 * columns], F32)
             words = raw_tiles[n][:].bitcast(F32).rearrange("p (r w) -> p r w", r=2)
-            nc.scalar.copy(
+            copy(
                 out=ordered[:].rearrange("p (r u c) -> p r u c", r=2, u=2),
-                in_=words[:, :, : 2 * count].rearrange("p r (c u) -> p r u c", u=2),
+                in_=words[:, :, : 2 * columns].rearrange("p r (c u) -> p r u c", u=2),
             )
-            ordered_tiles[n] = ordered
+            ordered_tiles[n] = (ordered, count)
 
         def transpose_and_regroup(n):
             words = raw_tiles[n][:].bitcast(F32)
+            ordered, ordered_count = ordered_tiles.get(n, (None, 0))
             grouped = grouped_pool.tile([P, PASSES * SLAB * 4], BF16, align_bytes=64)
             grouped_words = grouped[:].bitcast(F32).rearrange(
                 "p (g r c u) -> p g r c u", g=PASSES, r=2, u=2
@@ -83,9 +85,9 @@ def tile_attention_pa_kernel(tc, x, freq_cos, freq_sin, wq, wk, out_0, out_1):
                 turned = turned_pool.tile([P, 2, 2, P], F32)
                 for r in range(2):
                     for u in range(2):
-                        if n in ordered_tiles and g < ORDERED_PASSES:
-                            first = ((2 * r + u) * ORDERED_PASSES + g) * P
-                            source = ordered_tiles[n][:, first : first + P]
+                        if g < ordered_count:
+                            first = ((2 * r + u) * ordered_count + g) * P
+                            source = ordered[:, first : first + P]
                         else:
                             first = r * WORDS + 2 * g * P + u
                             source = words[:, first : first + 2 * P - 1 : 2]
@@ -210,25 +212,32 @@ def tile_attention_pa_kernel(tc, x, freq_cos, freq_sin, wq, wk, out_0, out_1):
 
         last = len(slabs) - 1
         waiting = None
+        late = []
         for n in range(X_SLABS, len(slabs)):
             if n - X_SLABS + RAW_BUFS <= last:
                 load(n - X_SLABS + RAW_BUFS)
             if n < last:
                 transpose_and_regroup(n + 1)
                 new_mx_tiles(n + 1)
-            if n + 3 <= last:
-                order_words(n + 3)
+            if FIRST_ORDERED <= n + 3 <= last:
+                order_words(n + 3, nc.scalar.copy, ordered_pool, ORDERED_PASSES)
             target = targets[n - X_SLABS]
             groups = [(0, 1), (2, 3)] if n < last else [(entry,) for entry in range(B)]
             products = [multiply(n, entries) for entries in groups]
             for part, entries in enumerate(groups):
                 if n < last:
                     quantise(n + 1, part)
+                if n == X_SLABS and part == 0:
+                    order_words(FIRST_ORDERED - 1, nc.vector.tensor_copy, keep, PASSES)
                 if waiting:
                     add_shared(*waiting)
                     waiting = None
                 factors = times_tables(products[part], entries)
                 if n < last:
                     waiting = (factors, entries, target)
+                elif part < B // 2:
+                    add_alone(nc.gpsimd, factors, entries, target)
                 else:
-                    add_alone(nc.gpsimd if part < B - 1 else nc.vector, factors, entries, target)
+                    late.append((factors, entries, target))
+        for sums in late:
+            add_alone(nc.vector, *sums)

@@ -14,8 +14,7 @@ ADD = mybir.AluOpType.add
 B, S, D, H, HD = 4, 128, 2048, 16, 128
 HALF = HD // 2
 P = 128
-K_PASS = 4 * P
-PASSES = D // K_PASS
+PASSES = D // (4 * P)
 WORDS = D // 2
 SLAB = 2 * P
 SLAB_HEADS = SLAB // HD
@@ -23,8 +22,10 @@ X_SLABS = B * S // SLAB
 W_SLABS = H * HD // SLAB
 BANK = 512
 ORDERED_PASSES = 3
-FIRST_ORDERED = X_SLABS + 3
+VECTOR_ORDERED = X_SLABS + 2
+FIRST_ORDERED = X_SLABS + 4
 RAW_BUFS = 9
+HALVED = 4
 OVERLAP = 8
 
 FLOPS = 2 * (B * S) * D * (2 * H * HD)
@@ -59,9 +60,13 @@ def tile_attention_pa_kernel(tc, x, freq_cos, freq_sin, wq, wk, out_0, out_1):
         def load(n):
             raw = raw_pool.tile([P, 2 * D], BF16)
             rows = raw[:].rearrange("p (r k) -> p r k", r=2)
-            width = K_PASS if n == 0 else D
-            for k in range(0, D, width):
-                nc.sync.dma_start(out=rows[:, :, k : k + width], in_=slabs[n][:, :, k : k + width])
+            if n < HALVED:
+                for k in (0, D // 2):
+                    for r in range(2):
+                        piece = slice(k, k + D // 2)
+                        nc.sync.dma_start(out=rows[:, r, piece], in_=slabs[n][:, r, piece])
+            else:
+                nc.sync.dma_start(out=rows, in_=slabs[n])
             raw_tiles[n] = raw
 
         def order_words(n, copy, pool, count):
@@ -228,7 +233,7 @@ def tile_attention_pa_kernel(tc, x, freq_cos, freq_sin, wq, wk, out_0, out_1):
                 if n < last:
                     quantise(n + 1, part)
                 if n == X_SLABS and part == 0:
-                    order_words(FIRST_ORDERED - 1, nc.vector.tensor_copy, keep, PASSES)
+                    order_words(VECTOR_ORDERED, nc.vector.tensor_copy, keep, PASSES)
                 if waiting:
                     add_shared(*waiting)
                     waiting = None

@@ -234,13 +234,15 @@ def tile_attention_pa_kernel(tc, x, freq_cos, freq_sin, wq, wk, out_0, out_1):
                     quantise(n + 1, part)
                 if n == X_SLABS and part == 0:
                     order_words(VECTOR_ORDERED, nc.vector.tensor_copy, keep, PASSES)
-                if waiting:
+                if waiting and n + part < last:
                     add_shared(*waiting)
-                    waiting = None
+                elif waiting:
+                    add_alone(nc.gpsimd, *waiting)
+                waiting = None
                 factors = times_tables(products[part], entries)
                 if n < last:
                     waiting = (factors, entries, target)
-                elif part < B // 2:
+                elif part == 0:
                     add_alone(nc.gpsimd, factors, entries, target)
                 else:
                     late.append((factors, entries, target))

from contextlib import ExitStack

import concourse.mybir as mybir
from concourse.masks import make_identity

F32 = mybir.dt.float32
BF16 = mybir.dt.bfloat16
U32 = mybir.dt.uint32
U8 = mybir.dt.uint8
FP8X4 = mybir.dt.float8_e4m3fn_x4
MULT = mybir.AluOpType.mult
ADD = mybir.AluOpType.add

B, S, D, H, HD = 4, 128, 2048, 16, 128
HALF = HD // 2
P = 128
PASSES = D // (4 * P)
WORDS = D // 2
SLAB = 2 * P
SLAB_HEADS = SLAB // HD
X_SLABS = B * S // SLAB
W_SLABS = H * HD // SLAB
BANK = 512
ORDERED_PASSES = 3
VECTOR_ORDERED = X_SLABS + 2
FIRST_ORDERED = X_SLABS + 4
RAW_BUFS = 9
HALVED = 4
OVERLAP = 8

FLOPS = 2 * (B * S) * D * (2 * H * HD)


def tile_attention_pa_kernel(tc, x, freq_cos, freq_sin, wq, wk, out_0, out_1):
    nc = tc.nc

    slabs = [x[2 * n : 2 * n + 2].rearrange("b s k -> s b k") for n in range(X_SLABS)]
    for w in (wq, wk):
        for n in range(W_SLABS):
            slabs.append(w[n * SLAB : (n + 1) * SLAB, :].rearrange("(c i) k -> c i k", i=2))
    targets = [(out, n * SLAB_HEADS) for out in (out_0, out_1) for n in range(W_SLABS)]

    with ExitStack() as ctx:
        keep = ctx.enter_context(tc.tile_pool(name="keep", bufs=1))
        raw_pool = ctx.enter_context(tc.tile_pool(name="raw", bufs=RAW_BUFS))
        ordered_pool = ctx.enter_context(tc.tile_pool(name="ordered", bufs=4))
        grouped_pool = ctx.enter_context(tc.tile_pool(name="grouped", bufs=3))
        w_pool = ctx.enter_context(tc.tile_pool(name="w_mx", bufs=3))
        rope_pool = ctx.enter_context(tc.tile_pool(name="rope", bufs=4))
        result_pool = ctx.enter_context(tc.tile_pool(name="result", bufs=8))
        turned_pool = ctx.enter_context(tc.psum_pool(name="turned", bufs=4))
        product_pool = ctx.enter_context(tc.psum_pool(name="product", bufs=4))
        ctx.enter_context(tc.manual_schedule())

        raw_tiles = {}
        ordered_tiles = {}
        grouped_tiles = {}
        mx_tiles = {}

        def load(n):
            raw = raw_pool.tile([P, 2 * D], BF16)
            rows = raw[:].rearrange("p (r k) -> p r k", r=2)
            if n < HALVED:
                for k in (0, D // 2):
                    for r in range(2):
                        piece = slice(k, k + D // 2)
                        nc.sync.dma_start(out=rows[:, r, piece], in_=slabs[n][:, r, piece])
            else:
                nc.sync.dma_start(out=rows, in_=slabs[n])
            raw_tiles[n] = raw

        def order_words(n, copy, pool, count):
            columns = count * P
            ordered = pool.tile([P, 2 * 2 * columns], F32)
            words = raw_tiles[n][:].bitcast(F32).rearrange("p (r w) -> p r w", r=2)
            copy(
                out=ordered[:].rearrange("p (r u c) -> p r u c", r=2, u=2),
                in_=words[:, :, : 2 * columns].rearrange("p r (c u) -> p r u c", u=2),
            )
            ordered_tiles[n] = (ordered, count)

        def transpose_and_regroup(n):
            words = raw_tiles[n][:].bitcast(F32)
            ordered, ordered_count = ordered_tiles.get(n, (None, 0))
            grouped = grouped_pool.tile([P, PASSES * SLAB * 4], BF16, align_bytes=64)
            grouped_words = grouped[:].bitcast(F32).rearrange(
                "p (g r c u) -> p g r c u", g=PASSES, r=2, u=2
            )
            for g in range(PASSES):
                turned = turned_pool.tile([P, 2, 2, P], F32)
                for r in range(2):
                    for u in range(2):
                        if g < ordered_count:
                            first = ((2 * r + u) * ordered_count + g) * P
                            source = ordered[:, first : first + P]
                        else:
                            first = r * WORDS + 2 * g * P + u
                            source = words[:, first : first + 2 * P - 1 : 2]
                        nc.tensor.transpose(turned[:, r, u, :], source, ident[:])
                nc.scalar.copy(out=grouped_words[:, g], in_=turned[:].rearrange("p r u c -> p r c u"))
            grouped_tiles[n] = grouped

        def new_mx_tiles(n):
            pool, label = (keep, "x%d" % n) if n < X_SLABS else (w_pool, "w")
            codes = pool.tile([P, PASSES * SLAB], U32, name=label + "_codes", align_bytes=64)
            scales = pool.tile([P, PASSES * SLAB], U8, name=label + "_scales", align_bytes=64)
            mx_tiles[n] = (codes, scales)

        def quantise(n, half):
            codes, scales = mx_tiles[n]
            cols = slice(half * 2 * SLAB, (half + 1) * 2 * SLAB)
            nc.vector.quantize_mx(
                out=codes[:, cols].bitcast(FP8X4),
                scales=scales[:, cols],
                in_=grouped_tiles[n][:, half * 8 * SLAB : (half + 1) * 8 * SLAB],
            )

        def multiply(n, entries):
            w_codes, w_scales = mx_tiles[n]
            product = product_pool.tile([P, BANK], F32)
            for place, entry in enumerate(entries):
                x_codes, x_scales = mx_tiles[entry // 2]
                for g in range(PASSES):
                    x_row = g * SLAB + entry % 2 * P
                    x_cols = slice(x_row, x_row + P)
                    w_cols = slice(g * SLAB, (g + 1) * SLAB)
                    nc.tensor.matmul_mx(
                        out=product[:, place * SLAB : (place + 1) * SLAB],
                        lhsT=x_codes[:, x_cols].bitcast(FP8X4),
                        lhsT_scale=x_scales[:, x_cols],
                        rhs=w_codes[:, w_cols].bitcast(FP8X4),
                        rhs_scale=w_scales[:, w_cols],
                        start=(g == 0),
                        stop=(g == PASSES - 1),
                    )
            return product

        def times_tables(product, entries):
            count = len(entries)
            cols = count * SLAB
            planes = product[:, :cols].rearrange("p (b i c) -> p b i c", b=count, i=2)
            twice = [P, count, P, 2]
            from_even = rope_pool.tile([P, BANK], F32)
            nc.vector.tensor_tensor(
                out=from_even[:, :cols].rearrange("p (b c i) -> p b c i", b=count, i=2),
                in0=planes[:, :, 0, :].unsqueeze(3).to_broadcast(twice),
                in1=cos_sin[:, :cols].rearrange("p (b c i) -> p b c i", b=count, i=2),
                op=MULT,
            )
            from_odd = rope_pool.tile([P, BANK], F32)
            nc.vector.tensor_tensor(
                out=from_odd[:, :cols].rearrange("p (b c i) -> p b c i", b=count, i=2),
                in0=planes[:, :, 1, :].unsqueeze(3).to_broadcast(twice),
                in1=minus_sin_cos[:, :cols].rearrange("p (b c i) -> p b c i", b=count, i=2),
                op=MULT,
            )
            return from_even, from_odd

        def store(rotated, entries, target):
            out, first_head = target
            for place, entry in enumerate(entries):
                nc.sync.dma_start(
                    out=out[entry, first_head : first_head + SLAB_HEADS].rearrange("h s d -> s h d"),
                    in_=rotated[:, place * SLAB : (place + 1) * SLAB].rearrange(
                        "p (h d) -> p h d", h=SLAB_HEADS
                    ),
                )

        def add_shared(factors, entries, target):
            from_even, from_odd = factors
            rotated = result_pool.tile([P, BANK], F32)
            for adder, cols in (
                (nc.vector, slice(0, SLAB + OVERLAP)),
                (nc.gpsimd, slice(SLAB, BANK)),
            ):
                adder.tensor_tensor(
                    out=rotated[:, cols], in0=from_even[:, cols], in1=from_odd[:, cols], op=ADD
                )
            store(rotated, entries, target)

        def add_alone(adder, factors, entries, target):
            from_even, from_odd = factors
            rotated = result_pool.tile([P, BANK], F32)
            cols = slice(0, len(entries) * SLAB)
            adder.tensor_tensor(
                out=rotated[:, cols], in0=from_even[:, cols], in1=from_odd[:, cols], op=ADD
            )
            store(rotated, entries, target)

        cos_bf = keep.tile([P, HALF], BF16)
        sin_bf = keep.tile([P, HALF], BF16)
        nc.scalar.dma_start(out=cos_bf[:], in_=freq_cos)
        nc.scalar.dma_start(out=sin_bf[:], in_=freq_sin)
        for n in range(RAW_BUFS):
            load(n)

        ident = keep.tile([P, P], F32)
        make_identity(nc, ident[:])

        repeats = BANK // HD
        cos_sin = keep.tile([P, BANK], F32)
        minus_sin_cos = keep.tile([P, BANK], F32)
        cos_sin_view = cos_sin[:].rearrange("p (n j i) -> p n j i", n=repeats, i=2)
        minus_sin_cos_view = minus_sin_cos[:].rearrange("p (n j i) -> p n j i", n=repeats, i=2)
        cos_repeated = cos_bf[:].unsqueeze(1).to_broadcast([P, repeats, HALF])
        sin_repeated = sin_bf[:].unsqueeze(1).to_broadcast([P, repeats, HALF])
        nc.vector.tensor_copy(out=cos_sin_view[:, :, :, 0], in_=cos_repeated)
        nc.vector.tensor_copy(out=cos_sin_view[:, :, :, 1], in_=sin_repeated)
        nc.vector.tensor_scalar_mul(out=minus_sin_cos_view[:, :, :, 0], in0=sin_repeated, scalar1=-1.0)
        nc.vector.tensor_copy(out=minus_sin_cos_view[:, :, :, 1], in_=cos_repeated)

        for n in range(X_SLABS + 1):
            transpose_and_regroup(n)
            new_mx_tiles(n)
            quantise(n, 0)
            quantise(n, 1)

        last = len(slabs) - 1
        waiting = None
        late = []
        for n in range(X_SLABS, len(slabs)):
            if n - X_SLABS + RAW_BUFS <= last:
                load(n - X_SLABS + RAW_BUFS)
            if n < last:
                transpose_and_regroup(n + 1)
                new_mx_tiles(n + 1)
            if FIRST_ORDERED <= n + 3 <= last:
                order_words(n + 3, nc.scalar.copy, ordered_pool, ORDERED_PASSES)
            target = targets[n - X_SLABS]
            groups = [(0, 1), (2, 3)] if n < last else [(entry,) for entry in range(B)]
            products = [multiply(n, entries) for entries in groups]
            for part, entries in enumerate(groups):
                if n < last:
                    quantise(n + 1, part)
                if n == X_SLABS and part == 0:
                    order_words(VECTOR_ORDERED, nc.vector.tensor_copy, keep, PASSES)
                if waiting and n + part < last:
                    add_shared(*waiting)
                elif waiting:
                    add_alone(nc.gpsimd, *waiting)
                waiting = None
                factors = times_tables(products[part], entries)
                if n < last:
                    waiting = (factors, entries, target)
                elif part == 0:
                    add_alone(nc.gpsimd, factors, entries, target)
                else:
                    late.append((factors, entries, target))
        for sums in late:
            add_alone(nc.vector, *sums)
